import numpy as np
import ml_dtypes


def mxq(x, axis, fmt="e4m3"):
    dtype, down = {"e4m3": (ml_dtypes.float8_e4m3fn, 7), "e5m2": (ml_dtypes.float8_e5m2, 14)}[fmt]
    v = np.moveaxis(np.asarray(x, np.float32).astype(ml_dtypes.bfloat16).astype(np.float64), axis, -1)
    blocks = v.reshape(v.shape[:-1] + (-1, 32))
    amax = np.abs(blocks).max(-1, keepdims=True)
    byte = np.maximum(np.where(amax > 0, np.frexp(amax)[1] - 1 + 127, 0) - down, 1)
    scale = np.exp2(byte - 127.0)
    codes = (blocks / scale).astype(np.float32).astype(dtype).astype(np.float64)
    return np.moveaxis((codes * scale).reshape(v.shape), -1, axis)


WIDE = False


def mx_kscale(k):
    if not WIDE:
        return np.ones(k)
    levels = np.array([10, -10, 5, -5, 0])
    a = np.random.permutation(np.resize(levels, k // 512 * 4)).reshape(k // 512, 4)
    idx = np.arange(k)
    return np.exp2(a[idx // 512, idx % 128 // 32])


BF16 = ml_dtypes.bfloat16


def bf(x):
    return np.asarray(x, np.float32).astype(BF16)


def f64(x):
    return np.asarray(x).astype(np.float64)


BS, CIN, H, D, L, P, OUT_DIM = 8, 512, 256, 1024, 10, 2, 128
K0, K1 = CIN * P, H * P


def patch_conv_relu(y, w):
    bs, cin, d = y.shape
    out, p = w.shape[0], w.shape[-1]
    q = d // p
    rows = y.reshape(bs, cin, q, p).transpose(0, 2, 1, 3).reshape(bs * q, cin * p)
    wm = w.reshape(out, cin * p).T
    z = (mxq(rows, 1, "e4m3") @ mxq(wm, 0, "e4m3")) * (1.0 / np.sqrt(cin))
    return np.maximum(z, 0.0).reshape(bs, q, out).transpose(0, 2, 1)


def setup_inputs():
    s = mx_kscale(K0).reshape(CIN, P)
    t = mx_kscale(K1)[::P]
    return {"x": bf(np.random.standard_normal((BS, CIN, D)) * np.tile(s, (1, D // P))),
            "w0": bf(np.random.standard_normal((H, CIN, P)) / s * t[:, None, None]),
            "w1": bf(np.random.standard_normal((H, H, P)) / t[:, None])}


def reference(x, w0, w1):
    h = patch_conv_relu(f64(x), f64(w0))
    return patch_conv_relu(h, f64(w1))

@@ -1,0 +1,184 @@
+import math
+from contextlib import ExitStack
+
+import concourse.mybir as mybir
+from concourse.masks import make_identity
+
+F32 = mybir.dt.float32
+BF16 = mybir.dt.bfloat16
+U32 = mybir.dt.uint32
+U8 = mybir.dt.uint8
+FP8X4 = mybir.dt.float8_e4m3fn_x4
+RELU = mybir.ActivationFunctionType.Relu
+
+P = 128
+BS, CIN, HID, D = 8, 512, 256, 1024
+Q = D // 2
+R = Q // 2
+FLOPS = 2 * BS * Q * HID * (2 * CIN) + 2 * BS * R * HID * (2 * HID)
+
+
+def tile_cnn_pa_t_kernel(tc, x, w0, w1, out):
+    nc = tc.nc
+    with ExitStack() as ctx:
+        const = ctx.enter_context(tc.tile_pool(name="const", bufs=1))
+        raw = ctx.enter_context(tc.tile_pool(name="raw", bufs=1))
+        work = ctx.enter_context(tc.tile_pool(name="work", bufs=3))
+        outs = ctx.enter_context(tc.tile_pool(name="outs", bufs=1))
+        ps_a = ctx.enter_context(tc.psum_pool(name="ps_a", bufs=5))
+        ps_b = ctx.enter_context(tc.psum_pool(name="ps_b", bufs=3))
+
+        xr = []
+        for b in range(BS):
+            xr_b = raw.tile([P, 4096], BF16, name="xr%d" % b)
+            xr.append(xr_b)
+        w0r = const.tile([P, 2048], BF16, name="w0r")
+        w1r = const.tile([P, 1024], BF16, name="w1r")
+
+        def load_x(b, gs):
+            src = x[b].rearrange("(g p r) d -> p g (r d)", g=2, p=P, r=2)
+            dst = xr[b][:].rearrange("p (g n) -> p g n", g=2)
+            if len(gs) == 2:
+                nc.sync.dma_start(out=dst, in_=src)
+            else:
+                nc.sync.dma_start(out=dst[:, gs[0], :], in_=src[:, gs[0], :])
+
+        load_x(0, [0])
+        load_x(0, [1])
+        nc.sync.dma_start(out=w0r[:], in_=w0.rearrange("(i m) c k -> i (m c k)", m=2))
+        nc.sync.dma_start(out=w1r[:], in_=w1.rearrange("(i m) c k -> i (m c k)", m=2))
+        for b in range(1, BS):
+            load_x(b, [0, 1])
+
+        warm = const.tile([P, 1], F32, name="warm")
+        nc.vector.memset(warm[:], 0.0)
+        nc.scalar.activation(out=warm[:], in_=warm[:], func=RELU)
+        ident = const.tile([P, P], F32, name="ident")
+        make_identity(nc, ident[:])
+
+        w0g = const.tile([P, 2048], BF16, name="w0g", align_bytes=64)
+        w0c = const.tile([P, 512], U32, name="w0c", align_bytes=64)
+        w0s = const.tile([P, 512], U8, name="w0s", align_bytes=64)
+        w1g = const.tile([P, 1024], BF16, name="w1g", align_bytes=64)
+        w1c = const.tile([P, 256], U32, name="w1c", align_bytes=64)
+        w1s = const.tile([P, 256], U8, name="w1s", align_bytes=64)
+
+        xg, xc, xs, hg, hc, hs, l1, l2, ot = {}, {}, {}, {}, {}, {}, {}, {}, {}
+
+        def regroup(b):
+            xg_b = work.tile([P, 4096], BF16, name="xg", align_bytes=64)
+            xg[b] = xg_b
+            src = xr[b][:].bitcast(F32).rearrange("p (g r h q) -> p g h q r", g=2, r=2, h=2)
+            dst = xg_b[:].bitcast(F32).rearrange("p (h g q r) -> p g h q r", h=2, g=2, r=2)
+            nc.vector.tensor_copy(out=dst[:, 0], in_=src[:, 0])
+            nc.vector.tensor_copy(out=dst[:, 1, 0], in_=src[:, 1, 0])
+            nc.scalar.copy(out=dst[:, 1, 1], in_=src[:, 1, 1])
+
+        def quant_x(b, h):
+            if h == 0:
+                xc_b = work.tile([P, 1024], U32, name="xc", align_bytes=64)
+                xs_b = work.tile([P, 1024], U8, name="xs", align_bytes=64)
+                xc[b] = xc_b
+                xs[b] = xs_b
+            nc.vector.quantize_mx(
+                out=xc[b][:, h * 512 : (h + 1) * 512].bitcast(FP8X4),
+                scales=xs[b][:, h * 512 : (h + 1) * 512],
+                in_=xg[b][:, h * 2048 : (h + 1) * 2048],
+            )
+
+        def layer1(b, h):
+            bank = ps_a.tile([P, 512], F32, name="bank_a")
+            l1[(b, h)] = bank
+            for m in range(2):
+                for g in range(2):
+                    wsl = slice((g * 2 + m) * P, (g * 2 + m + 1) * P)
+                    xsl = slice(h * 512 + g * 256, h * 512 + (g + 1) * 256)
+                    nc.tensor.matmul_mx(
+                        out=bank[:, m * 256 : (m + 1) * 256],
+                        lhsT=w0c[:, wsl].bitcast(FP8X4),
+                        lhsT_scale=w0s[:, wsl],
+                        rhs=xc[b][:, xsl].bitcast(FP8X4),
+                        rhs_scale=xs[b][:, xsl],
+                        start=(g == 0),
+                        stop=(g == 1),
+                    )
+
+        def evac_h(b, h):
+            if h == 0:
+                hg_b = work.tile([P, 1024], BF16, name="hg", align_bytes=64)
+                hg[b] = hg_b
+            nc.scalar.activation(
+                out=hg[b][:, h * 512 : (h + 1) * 512].rearrange("p (r m e) -> p r m e", m=2, e=2),
+                in_=l1[(b, h)][:].rearrange("p (m r e) -> p r m e", m=2, e=2),
+                func=RELU,
+                scale=1.0 / math.sqrt(float(CIN)),
+            )
+
+        def quant_h(b):
+            hc_b = work.tile([P, 256], U32, name="hc", align_bytes=64)
+            hs_b = work.tile([P, 256], U8, name="hs", align_bytes=64)
+            hc[b] = hc_b
+            hs[b] = hs_b
+            nc.vector.quantize_mx(out=hc_b[:].bitcast(FP8X4), scales=hs_b[:], in_=hg[b][:])
+
+        def layer2(b):
+            bank = ps_b.tile([P, 512], F32, name="bank_b")
+            l2[b] = bank
+            for m in range(2):
+                nc.tensor.matmul_mx(
+                    out=bank[:, m * 256 : (m + 1) * 256],
+                    lhsT=w1c[:, m * P : (m + 1) * P].bitcast(FP8X4),
+                    lhsT_scale=w1s[:, m * P : (m + 1) * P],
+                    rhs=hc[b][:].bitcast(FP8X4),
+                    rhs_scale=hs[b][:],
+                    start=True,
+                    stop=True,
+                )
+
+        def evac_o(b):
+            ot_b = outs.tile([P, 512], F32, name="ot%d" % b)
+            nc.scalar.activation(out=ot_b[:], in_=l2[b][:], func=RELU, scale=1.0 / math.sqrt(float(HID)))
+            nc.sync.dma_start(out=out[b].rearrange("(i m) r -> i (m r)", m=2), in_=ot_b[:])
+
+        def weights():
+            w0w = w0r[:].bitcast(F32).rearrange("i (m g p u) -> i m g u p", m=2, g=2, u=2)
+            w0gw = w0g[:].bitcast(F32).rearrange("p (g m i u) -> p g m i u", g=2, m=2, u=2)
+            for g in range(2):
+                tw = ps_a.tile([P, 512], F32, name="bank_a")
+                for m in range(2):
+                    for u in range(2):
+                        s = 2 * m + u
+                        nc.tensor.transpose(tw[:, s * P : (s + 1) * P], w0w[:, m, g, u, :], ident[:])
+                nc.scalar.copy(out=w0gw[:, g], in_=tw[:].rearrange("p (m u i) -> p m i u", m=2, u=2))
+            w1w = w1r[:].bitcast(F32).rearrange("i (m p u) -> i m u p", m=2, u=2)
+            w1gw = w1g[:].bitcast(F32).rearrange("p (m i u) -> p m i u", m=2, u=2)
+            tw = ps_a.tile([P, 512], F32, name="bank_a")
+            for m in range(2):
+                for u in range(2):
+                    s = 2 * m + u
+                    nc.tensor.transpose(tw[:, s * P : (s + 1) * P], w1w[:, m, u, :], ident[:])
+            nc.scalar.copy(out=w1gw, in_=tw[:].rearrange("p (m u i) -> p m i u", m=2, u=2))
+            nc.vector.quantize_mx(out=w0c[:].bitcast(FP8X4), scales=w0s[:], in_=w0g[:])
+            nc.vector.quantize_mx(out=w1c[:].bitcast(FP8X4), scales=w1s[:], in_=w1g[:])
+
+        for t in range(BS + 2):
+            if t < BS:
+                regroup(t)
+            if 1 <= t <= BS:
+                evac_h(t - 1, 0)
+                evac_h(t - 1, 1)
+            if t < BS:
+                quant_x(t, 0)
+                if t == 0:
+                    quant_x(t, 1)
+                    weights()
+                    layer1(t, 0)
+                else:
+                    layer1(t, 0)
+                    quant_x(t, 1)
+                layer1(t, 1)
+            if 1 <= t <= BS:
+                quant_h(t - 1)
+                layer2(t - 1)
+            if t >= 2:
+                evac_o(t - 2)

@@ -10,12 +10,16 @@ U32 = mybir.dt.uint32
 U8 = mybir.dt.uint8
 FP8X4 = mybir.dt.float8_e4m3fn_x4
 RELU = mybir.ActivationFunctionType.Relu
+MULT = mybir.AluOpType.mult
+MAX = mybir.AluOpType.max
 
 P = 128
 BS, CIN, HID, D = 8, 512, 256, 1024
 Q = D // 2
 R = Q // 2
 FLOPS = 2 * BS * Q * HID * (2 * CIN) + 2 * BS * R * HID * (2 * HID)
+S1 = 1.0 / math.sqrt(float(CIN))
+S2 = 1.0 / math.sqrt(float(HID))
 
 
 def tile_cnn_pa_t_kernel(tc, x, w0, w1, out):
@@ -23,7 +27,7 @@ def tile_cnn_pa_t_kernel(tc, x, w0, w1, out):
     with ExitStack() as ctx:
         const = ctx.enter_context(tc.tile_pool(name="const", bufs=1))
         raw = ctx.enter_context(tc.tile_pool(name="raw", bufs=1))
-        work = ctx.enter_context(tc.tile_pool(name="work", bufs=3))
+        work = ctx.enter_context(tc.tile_pool(name="work", bufs=4))
         outs = ctx.enter_context(tc.tile_pool(name="outs", bufs=1))
         ps_a = ctx.enter_context(tc.psum_pool(name="ps_a", bufs=5))
         ps_b = ctx.enter_context(tc.psum_pool(name="ps_b", bufs=3))
@@ -35,20 +39,25 @@ def tile_cnn_pa_t_kernel(tc, x, w0, w1, out):
         w0r = const.tile([P, 2048], BF16, name="w0r")
         w1r = const.tile([P, 1024], BF16, name="w1r")
 
-        def load_x(b, gs):
-            src = x[b].rearrange("(g p r) d -> p g (r d)", g=2, p=P, r=2)
-            dst = xr[b][:].rearrange("p (g n) -> p g n", g=2)
-            if len(gs) == 2:
-                nc.sync.dma_start(out=dst, in_=src)
-            else:
-                nc.sync.dma_start(out=dst[:, gs[0], :], in_=src[:, gs[0], :])
+        def load_batch(b):
+            nc.sync.dma_start(
+                out=xr[b][:].rearrange("p (g n) -> p g n", g=2),
+                in_=x[b].rearrange("(g p r) d -> p g (r d)", g=2, p=P, r=2),
+            )
 
-        load_x(0, [0])
-        load_x(0, [1])
+        def load_piece(b, g, h):
+            nc.sync.dma_start(
+                out=xr[b][:].rearrange("p (g r h e) -> p g r h e", g=2, r=2, h=2)[:, g, :, h, :],
+                in_=x[b].rearrange("(g p r) (h e) -> g h p r e", g=2, p=P, r=2, h=2)[g, h],
+            )
+
         nc.sync.dma_start(out=w0r[:], in_=w0.rearrange("(i m) c k -> i (m c k)", m=2))
+        for h in range(2):
+            for g in range(2):
+                load_piece(0, g, h)
         nc.sync.dma_start(out=w1r[:], in_=w1.rearrange("(i m) c k -> i (m c k)", m=2))
         for b in range(1, BS):
-            load_x(b, [0, 1])
+            load_batch(b)
 
         warm = const.tile([P, 1], F32, name="warm")
         nc.vector.memset(warm[:], 0.0)
@@ -63,18 +72,42 @@ def tile_cnn_pa_t_kernel(tc, x, w0, w1, out):
         w1c = const.tile([P, 256], U32, name="w1c", align_bytes=64)
         w1s = const.tile([P, 256], U8, name="w1s", align_bytes=64)
 
-        xg, xc, xs, hg, hc, hs, l1, l2, ot = {}, {}, {}, {}, {}, {}, {}, {}, {}
+        xg, xc, xs, hg, hc, hs, l1, l2, ot, tw = {}, {}, {}, {}, {}, {}, {}, {}, {}, {}
 
-        def regroup(b):
-            xg_b = work.tile([P, 4096], BF16, name="xg", align_bytes=64)
-            xg[b] = xg_b
-            src = xr[b][:].bitcast(F32).rearrange("p (g r h q) -> p g h q r", g=2, r=2, h=2)
-            dst = xg_b[:].bitcast(F32).rearrange("p (h g q r) -> p g h q r", h=2, g=2, r=2)
-            nc.vector.tensor_copy(out=dst[:, 0], in_=src[:, 0])
-            nc.vector.tensor_copy(out=dst[:, 1, 0], in_=src[:, 1, 0])
-            nc.scalar.copy(out=dst[:, 1, 1], in_=src[:, 1, 1])
+        def relu_out(eng, dst, src, scale):
+            if eng == "S":
+                nc.scalar.activation(out=dst, in_=src, func=RELU, scale=scale)
+            else:
+                nc.vector.tensor_scalar(out=dst, in0=src, scalar1=scale, scalar2=0.0, op0=MULT, op1=MAX)
 
-        def quant_x(b, h):
+        def copy_words(eng, dst, src):
+            if eng == "S":
+                nc.scalar.copy(out=dst, in_=src)
+            else:
+                nc.vector.tensor_copy(out=dst, in_=src)
+
+        def views(b):
+            if b not in xg:
+                xg_b = work.tile([P, 4096], BF16, name="xg", align_bytes=64)
+                xg[b] = xg_b
+            src = xr[b][:].bitcast(F32).rearrange("p (g r h q) -> p h g q r", g=2, r=2, h=2)
+            dst = xg[b][:].bitcast(F32).rearrange("p (h g q r) -> p h g q r", h=2, g=2, r=2)
+            return src, dst
+
+        def ra(b):
+            src, dst = views(b)
+            copy_words("V", dst[:, 0], src[:, 0])
+
+        def rb(b):
+            src, dst = views(b)
+            copy_words("V", dst[:, 1, 0], src[:, 1, 0])
+
+        def rs(b):
+            src, dst = views(b)
+            copy_words("S", dst[:, 1, 1], src[:, 1, 1])
+
+        def qx(c):
+            b, h = divmod(c, 2)
             if h == 0:
                 xc_b = work.tile([P, 1024], U32, name="xc", align_bytes=64)
                 xs_b = work.tile([P, 1024], U8, name="xs", align_bytes=64)
@@ -86,9 +119,10 @@ def tile_cnn_pa_t_kernel(tc, x, w0, w1, out):
                 in_=xg[b][:, h * 2048 : (h + 1) * 2048],
             )
 
-        def layer1(b, h):
+        def m1(c):
+            b, h = divmod(c, 2)
             bank = ps_a.tile([P, 512], F32, name="bank_a")
-            l1[(b, h)] = bank
+            l1[c] = bank
             for m in range(2):
                 for g in range(2):
                     wsl = slice((g * 2 + m) * P, (g * 2 + m + 1) * P)
@@ -103,82 +137,132 @@ def tile_cnn_pa_t_kernel(tc, x, w0, w1, out):
                         stop=(g == 1),
                     )
 
-        def evac_h(b, h):
+        def eh(c, eng):
+            b, h = divmod(c, 2)
             if h == 0:
                 hg_b = work.tile([P, 1024], BF16, name="hg", align_bytes=64)
                 hg[b] = hg_b
-            nc.scalar.activation(
-                out=hg[b][:, h * 512 : (h + 1) * 512].rearrange("p (r m e) -> p r m e", m=2, e=2),
-                in_=l1[(b, h)][:].rearrange("p (m r e) -> p r m e", m=2, e=2),
-                func=RELU,
-                scale=1.0 / math.sqrt(float(CIN)),
+            relu_out(
+                eng,
+                hg[b][:, h * 512 : (h + 1) * 512].rearrange("p (r m e) -> p r m e", m=2, e=2),
+                l1[c][:].rearrange("p (m r e) -> p r m e", m=2, e=2),
+                S1,
             )
 
-        def quant_h(b):
-            hc_b = work.tile([P, 256], U32, name="hc", align_bytes=64)
-            hs_b = work.tile([P, 256], U8, name="hs", align_bytes=64)
-            hc[b] = hc_b
-            hs[b] = hs_b
-            nc.vector.quantize_mx(out=hc_b[:].bitcast(FP8X4), scales=hs_b[:], in_=hg[b][:])
+        def q2(b, hs_list):
+            if b not in hc:
+                hc_b = work.tile([P, 256], U32, name="hc", align_bytes=64)
+                hs_b = work.tile([P, 256], U8, name="hs", align_bytes=64)
+                hc[b] = hc_b
+                hs[b] = hs_b
+            lo, hi = hs_list[0] * 128, (hs_list[-1] + 1) * 128
+            nc.vector.quantize_mx(
+                out=hc[b][:, lo:hi].bitcast(FP8X4), scales=hs[b][:, lo:hi], in_=hg[b][:, 4 * lo : 4 * hi]
+            )
 
-        def layer2(b):
-            bank = ps_b.tile([P, 512], F32, name="bank_b")
-            l2[b] = bank
+        def m2(b, hs_list):
+            lo, hi = hs_list[0] * 128, (hs_list[-1] + 1) * 128
+            n = hi - lo
+            bank = ps_b.tile([P, 2 * n], F32, name="bank_b")
+            l2[(b, hs_list[0])] = bank
             for m in range(2):
                 nc.tensor.matmul_mx(
-                    out=bank[:, m * 256 : (m + 1) * 256],
+                    out=bank[:, m * n : (m + 1) * n],
                     lhsT=w1c[:, m * P : (m + 1) * P].bitcast(FP8X4),
                     lhsT_scale=w1s[:, m * P : (m + 1) * P],
-                    rhs=hc[b][:].bitcast(FP8X4),
-                    rhs_scale=hs[b][:],
+                    rhs=hc[b][:, lo:hi].bitcast(FP8X4),
+                    rhs_scale=hs[b][:, lo:hi],
                     start=True,
                     stop=True,
                 )
 
-        def evac_o(b):
-            ot_b = outs.tile([P, 512], F32, name="ot%d" % b)
-            nc.scalar.activation(out=ot_b[:], in_=l2[b][:], func=RELU, scale=1.0 / math.sqrt(float(HID)))
-            nc.sync.dma_start(out=out[b].rearrange("(i m) r -> i (m r)", m=2), in_=ot_b[:])
+        def eo(b, hs_list, eng):
+            if b not in ot:
+                ot_b = outs.tile([P, 512], F32, name="ot%d" % b)
+                ot[b] = ot_b
+            lo, hi = hs_list[0] * 128, (hs_list[-1] + 1) * 128
+            dst = ot[b][:].rearrange("p (m r) -> p m r", m=2)[:, :, lo:hi]
+            relu_out(eng, dst, l2[(b, hs_list[0])][:].rearrange("p (m r) -> p m r", m=2), S2)
+            nc.sync.dma_start(out=out[b].rearrange("(i m) r -> i m r", m=2)[:, :, lo:hi], in_=dst)
 
-        def weights():
-            w0w = w0r[:].bitcast(F32).rearrange("i (m g p u) -> i m g u p", m=2, g=2, u=2)
-            w0gw = w0g[:].bitcast(F32).rearrange("p (g m i u) -> p g m i u", g=2, m=2, u=2)
-            for g in range(2):
-                tw = ps_a.tile([P, 512], F32, name="bank_a")
-                for m in range(2):
-                    for u in range(2):
-                        s = 2 * m + u
-                        nc.tensor.transpose(tw[:, s * P : (s + 1) * P], w0w[:, m, g, u, :], ident[:])
-                nc.scalar.copy(out=w0gw[:, g], in_=tw[:].rearrange("p (m u i) -> p m i u", m=2, u=2))
-            w1w = w1r[:].bitcast(F32).rearrange("i (m p u) -> i m u p", m=2, u=2)
-            w1gw = w1g[:].bitcast(F32).rearrange("p (m i u) -> p m i u", m=2, u=2)
-            tw = ps_a.tile([P, 512], F32, name="bank_a")
+        w0w = w0r[:].bitcast(F32).rearrange("i (m g p u) -> i m g u p", m=2, g=2, u=2)
+        w0gw = w0g[:].bitcast(F32).rearrange("p (g m i u) -> p g m i u", g=2, m=2, u=2)
+        w1w = w1r[:].bitcast(F32).rearrange("i (m p u) -> i m u p", m=2, u=2)
+        w1gw = w1g[:].bitcast(F32).rearrange("p (m i u) -> p m i u", m=2, u=2)
+
+        def tw0(g):
+            bank = ps_a.tile([P, 512], F32, name="bank_a")
+            tw[g] = bank
             for m in range(2):
                 for u in range(2):
                     s = 2 * m + u
-                    nc.tensor.transpose(tw[:, s * P : (s + 1) * P], w1w[:, m, u, :], ident[:])
-            nc.scalar.copy(out=w1gw, in_=tw[:].rearrange("p (m u i) -> p m i u", m=2, u=2))
+                    nc.tensor.transpose(bank[:, s * P : (s + 1) * P], w0w[:, m, g, u, :], ident[:])
+
+        def ew0(g, eng):
+            copy_words(eng, w0gw[:, g], tw[g][:].rearrange("p (m u i) -> p m i u", m=2, u=2))
+
+        def tw1():
+            bank = ps_a.tile([P, 512], F32, name="bank_a")
+            tw[2] = bank
+            for m in range(2):
+                for u in range(2):
+                    s = 2 * m + u
+                    nc.tensor.transpose(bank[:, s * P : (s + 1) * P], w1w[:, m, u, :], ident[:])
+
+        def ew1(eng):
+            copy_words(eng, w1gw, tw[2][:].rearrange("p (m u i) -> p m i u", m=2, u=2))
+
+        def qw0():
             nc.vector.quantize_mx(out=w0c[:].bitcast(FP8X4), scales=w0s[:], in_=w0g[:])
+
+        def qw1():
             nc.vector.quantize_mx(out=w1c[:].bitcast(FP8X4), scales=w1s[:], in_=w1g[:])
 
-        for t in range(BS + 2):
-            if t < BS:
-                regroup(t)
-            if 1 <= t <= BS:
-                evac_h(t - 1, 0)
-                evac_h(t - 1, 1)
-            if t < BS:
-                quant_x(t, 0)
-                if t == 0:
-                    quant_x(t, 1)
-                    weights()
-                    layer1(t, 0)
-                else:
-                    layer1(t, 0)
-                    quant_x(t, 1)
-                layer1(t, 1)
-            if 1 <= t <= BS:
-                quant_h(t - 1)
-                layer2(t - 1)
-            if t >= 2:
-                evac_o(t - 2)
+        ctx.enter_context(tc.manual_schedule())
+        BOTH = [0, 1]
+        tw0(0)
+        tw0(1)
+        ew0(0, "S")
+        ra(0)
+        ew0(1, "V")
+        rb(0)
+        rs(0)
+        qw0()
+        tw1()
+        ew1("S")
+        qx(0)
+        m1(0)
+        qx(1)
+        m1(1)
+        for p in range(1, BS):
+            ra(p)
+            rs(p)
+            rb(p)
+            qx(2 * p)
+            m1(2 * p)
+            qx(2 * p + 1)
+            m1(2 * p + 1)
+            if p == 1:
+                qw1()
+            eh(2 * p - 2, "S")
+            eh(2 * p - 1, "S")
+            if 2 <= p < BS - 1:
+                q2(p - 2, BOTH)
+                m2(p - 2, BOTH)
+            if 3 <= p < BS - 1:
+                eo(p - 3, BOTH, "S")
+        q2(5, BOTH)
+        m2(5, BOTH)
+        eo(4, BOTH, "V")
+        eh(14, "S")
+        q2(6, BOTH)
+        m2(6, BOTH)
+        eh(15, "V")
+        q2(7, [0])
+        m2(7, [0])
+        eo(5, BOTH, "S")
+        q2(7, [1])
+        m2(7, [1])
+        eo(6, BOTH, "S")
+        eo(7, [0], "S")
+        eo(7, [1], "V")

@@ -21,14 +21,43 @@ FLOPS = 2 * BS * Q * HID * (2 * CIN) + 2 * BS * R * HID * (2 * HID)
 S1 = 1.0 / math.sqrt(float(CIN))
 S2 = 1.0 / math.sqrt(float(HID))
 
+LOADS = [("g", 0, 0), ("w0", 0, 0), ("g", 0, 1), ("w1", 0, 0), ("g", 1, 0), ("g", 1, 1), ("g", 2, 0), ("g", 2, 1), ("g", 3, 0), ("g", 3, 1), ("g", 4, 0), ("g", 4, 1), ("g", 5, 0), ("g", 5, 1), ("g", 6, 0), ("g", 6, 1), ("g", 7, 0), ("g", 7, 1)]
+ORDER = [
+    ("r", 0, 0, "V"), ("qx", 0, 0, ""), ("tw0", 0, 0, ""), ("tw0", 1, 0, ""), ("ew0", 0, 0, "S"), ("ew0", 1, 0, "S"),
+    ("r", 0, 1, "V"), ("qx", 0, 1, ""), ("tw1", 0, 0, ""), ("r", 1, 0, "V"), ("r", 1, 0, "S"), ("qw0", 0, 0, ""),
+    ("m1", 0, 0, ""), ("m1", 1, 0, ""), ("ew1", 0, 0, "S"), ("r", 1, 1, "V"), ("r", 1, 1, "S"), ("qx", 1, 0, ""),
+    ("r", 2, 0, "V"), ("r", 2, 0, "S"), ("eh", 0, 0, "S"), ("qx", 1, 1, ""), ("m1", 2, 0, ""), ("m1", 3, 0, ""),
+    ("r", 2, 1, "V"), ("r", 2, 1, "S"), ("eh", 1, 0, "S"), ("qx", 2, 0, ""), ("r", 3, 0, "V"), ("r", 3, 0, "S"),
+    ("eh", 2, 0, "S"), ("qx", 2, 1, ""), ("m1", 4, 0, ""), ("m1", 5, 0, ""), ("qw1", 0, 0, ""), ("r", 3, 1, "V"),
+    ("r", 3, 1, "S"), ("eh", 3, 0, "S"), ("qx", 3, 0, ""), ("r", 4, 0, "V"), ("r", 4, 0, "S"), ("eh", 4, 0, "S"),
+    ("qx", 3, 1, ""), ("m1", 6, 0, ""), ("m1", 7, 0, ""), ("q2", 0, 2, ""), ("m2", 0, 2, ""), ("r", 4, 1, "V"),
+    ("r", 4, 1, "S"), ("eh", 5, 0, "S"), ("qx", 4, 0, ""), ("r", 5, 0, "V"), ("r", 5, 0, "S"), ("eh", 6, 0, "S"),
+    ("qx", 4, 1, ""), ("m1", 8, 0, ""), ("m1", 9, 0, ""), ("q2", 1, 2, ""), ("m2", 1, 2, ""), ("r", 5, 1, "V"),
+    ("r", 5, 1, "S"), ("eh", 7, 0, "S"), ("qx", 5, 0, ""), ("eo", 0, 2, "S"), ("st", 0, 2, ""), ("r", 6, 0, "V"),
+    ("r", 6, 0, "S"), ("eh", 8, 0, "S"), ("qx", 5, 1, ""), ("m1", 10, 0, ""), ("m1", 11, 0, ""), ("q2", 2, 2, ""),
+    ("m2", 2, 2, ""), ("r", 6, 1, "V"), ("r", 6, 1, "S"), ("eh", 9, 0, "S"), ("qx", 6, 0, ""), ("r", 7, 0, "V"),
+    ("r", 7, 0, "S"), ("eh", 10, 0, "S"), ("qx", 6, 1, ""), ("m1", 12, 0, ""), ("m1", 13, 0, ""), ("q2", 3, 2, ""),
+    ("m2", 3, 2, ""), ("r", 7, 1, "V"), ("r", 7, 1, "S"), ("eh", 11, 0, "S"), ("qx", 7, 0, ""), ("qxh", 7, 1, "a"),
+    ("m1", 14, 0, ""), ("qxh", 7, 1, "b"), ("m1", 15, 0, ""), ("eo", 1, 2, "S"), ("eo", 2, 2, "V"), ("eh", 12, 0, "S"),
+    ("q2", 4, 2, ""), ("st", 1, 2, ""), ("eh", 13, 0, "S"), ("q2", 5, 2, ""), ("st", 2, 2, ""), ("eh", 14, 0, "S"),
+    ("eo", 3, 2, "V"), ("m2", 4, 2, ""), ("m2", 5, 2, ""), ("q2", 6, 2, ""), ("eh", 15, 0, "S"), ("eo", 4, 2, "V"),
+    ("st", 3, 2, ""), ("eo", 5, 2, "S"), ("m2", 6, 2, ""), ("q2", 7, 0, ""), ("q2", 7, 1, ""), ("st", 4, 2, ""),
+    ("m2", 7, 0, ""), ("eo", 6, 2, "S"), ("m2", 7, 1, ""), ("st", 5, 2, ""), ("eo", 7, 0, "S"), ("eo", 7, 1, "V"),
+    ("st", 6, 2, ""), ("st", 7, 0, ""), ("st", 7, 1, ""),
+]
+
+
+def scalar_words(b, g):
+    return 0 if b == 0 else (512 if (b == 7 and g == 1) else 384)
+
 
 def tile_cnn_pa_t_kernel(tc, x, w0, w1, out):
     nc = tc.nc
     with ExitStack() as ctx:
         const = ctx.enter_context(tc.tile_pool(name="const", bufs=1))
         raw = ctx.enter_context(tc.tile_pool(name="raw", bufs=1))
-        work = ctx.enter_context(tc.tile_pool(name="work", bufs=4))
-        outs = ctx.enter_context(tc.tile_pool(name="outs", bufs=1))
+        work = ctx.enter_context(tc.tile_pool(name="work", bufs=3))
+        hid = ctx.enter_context(tc.tile_pool(name="hid", bufs=1))
         ps_a = ctx.enter_context(tc.psum_pool(name="ps_a", bufs=5))
         ps_b = ctx.enter_context(tc.psum_pool(name="ps_b", bufs=3))
 
@@ -39,25 +68,21 @@ def tile_cnn_pa_t_kernel(tc, x, w0, w1, out):
         w0r = const.tile([P, 2048], BF16, name="w0r")
         w1r = const.tile([P, 1024], BF16, name="w1r")
 
-        def load_batch(b):
-            nc.sync.dma_start(
-                out=xr[b][:].rearrange("p (g n) -> p g n", g=2),
-                in_=x[b].rearrange("(g p r) d -> p g (r d)", g=2, p=P, r=2),
-            )
-
-        def load_piece(b, g, h):
-            nc.sync.dma_start(
-                out=xr[b][:].rearrange("p (g r h e) -> p g r h e", g=2, r=2, h=2)[:, g, :, h, :],
-                in_=x[b].rearrange("(g p r) (h e) -> g h p r e", g=2, p=P, r=2, h=2)[g, h],
-            )
-
-        nc.sync.dma_start(out=w0r[:], in_=w0.rearrange("(i m) c k -> i (m c k)", m=2))
-        for h in range(2):
-            for g in range(2):
-                load_piece(0, g, h)
-        nc.sync.dma_start(out=w1r[:], in_=w1.rearrange("(i m) c k -> i (m c k)", m=2))
-        for b in range(1, BS):
-            load_batch(b)
+        for kind, b, g in LOADS:
+            if kind == "w0":
+                nc.sync.dma_start(out=w0r[:], in_=w0.rearrange("(i m) c k -> i (m c k)", m=2))
+            elif kind == "w1":
+                nc.sync.dma_start(out=w1r[:], in_=w1.rearrange("(i m) c k -> i (m c k)", m=2))
+            elif kind == "g":
+                nc.sync.dma_start(
+                    out=xr[b][:, g * 2048 : (g + 1) * 2048],
+                    in_=x[b].rearrange("(g p r) d -> g p (r d)", g=2, p=P, r=2)[g],
+                )
+            else:
+                nc.sync.dma_start(
+                    out=xr[b][:].rearrange("p (g n) -> p g n", g=2),
+                    in_=x[b].rearrange("(g p r) d -> p g (r d)", g=2, p=P, r=2),
+                )
 
         warm = const.tile([P, 1], F32, name="warm")
         nc.vector.memset(warm[:], 0.0)
@@ -86,37 +111,24 @@ def tile_cnn_pa_t_kernel(tc, x, w0, w1, out):
             else:
                 nc.vector.tensor_copy(out=dst, in_=src)
 
-        def views(b):
+        def regroup(b, g, eng):
             if b not in xg:
                 xg_b = work.tile([P, 4096], BF16, name="xg", align_bytes=64)
                 xg[b] = xg_b
-            src = xr[b][:].bitcast(F32).rearrange("p (g r h q) -> p h g q r", g=2, r=2, h=2)
-            dst = xg[b][:].bitcast(F32).rearrange("p (h g q r) -> p h g q r", h=2, g=2, r=2)
-            return src, dst
+            cut = Q - scalar_words(b, g) // 2
+            lo, hi = (0, cut) if eng == "V" else (cut, Q)
+            src = xr[b][:].bitcast(F32).rearrange("p (g r q) -> p g q r", g=2, r=2)
+            dst = xg[b][:].bitcast(F32).rearrange("p (g q r) -> p g q r", g=2, r=2)
+            copy_words(eng, dst[:, g, lo:hi, :], src[:, g, lo:hi, :])
 
-        def ra(b):
-            src, dst = views(b)
-            copy_words("V", dst[:, 0], src[:, 0])
-
-        def rb(b):
-            src, dst = views(b)
-            copy_words("V", dst[:, 1, 0], src[:, 1, 0])
-
-        def rs(b):
-            src, dst = views(b)
-            copy_words("S", dst[:, 1, 1], src[:, 1, 1])
-
-        def qx(c):
-            b, h = divmod(c, 2)
-            if h == 0:
+        def quant_x(b, lo, hi):
+            if b not in xc:
                 xc_b = work.tile([P, 1024], U32, name="xc", align_bytes=64)
                 xs_b = work.tile([P, 1024], U8, name="xs", align_bytes=64)
                 xc[b] = xc_b
                 xs[b] = xs_b
             nc.vector.quantize_mx(
-                out=xc[b][:, h * 512 : (h + 1) * 512].bitcast(FP8X4),
-                scales=xs[b][:, h * 512 : (h + 1) * 512],
-                in_=xg[b][:, h * 2048 : (h + 1) * 2048],
+                out=xc[b][:, lo:hi].bitcast(FP8X4), scales=xs[b][:, lo:hi], in_=xg[b][:, 4 * lo : 4 * hi]
             )
 
         def m1(c):
@@ -126,7 +138,7 @@ def tile_cnn_pa_t_kernel(tc, x, w0, w1, out):
             for m in range(2):
                 for g in range(2):
                     wsl = slice((g * 2 + m) * P, (g * 2 + m + 1) * P)
-                    xsl = slice(h * 512 + g * 256, h * 512 + (g + 1) * 256)
+                    xsl = slice(g * 512 + h * 256, g * 512 + (h + 1) * 256)
                     nc.tensor.matmul_mx(
                         out=bank[:, m * 256 : (m + 1) * 256],
                         lhsT=w0c[:, wsl].bitcast(FP8X4),
@@ -139,8 +151,8 @@ def tile_cnn_pa_t_kernel(tc, x, w0, w1, out):
 
         def eh(c, eng):
             b, h = divmod(c, 2)
-            if h == 0:
-                hg_b = work.tile([P, 1024], BF16, name="hg", align_bytes=64)
+            if b not in hg:
+                hg_b = hid.tile([P, 1024], BF16, name="hg%d" % b, align_bytes=64)
                 hg[b] = hg_b
             relu_out(
                 eng,
@@ -149,22 +161,25 @@ def tile_cnn_pa_t_kernel(tc, x, w0, w1, out):
                 S1,
             )
 
-        def q2(b, hs_list):
+        def span(part):
+            return (0, 256) if part == 2 else (part * 128, (part + 1) * 128)
+
+        def q2(b, part):
             if b not in hc:
-                hc_b = work.tile([P, 256], U32, name="hc", align_bytes=64)
-                hs_b = work.tile([P, 256], U8, name="hs", align_bytes=64)
+                hc_b = hid.tile([P, 256], U32, name="hc%d" % b, align_bytes=64)
+                hs_b = hid.tile([P, 256], U8, name="hs%d" % b, align_bytes=64)
                 hc[b] = hc_b
                 hs[b] = hs_b
-            lo, hi = hs_list[0] * 128, (hs_list[-1] + 1) * 128
+            lo, hi = span(part)
             nc.vector.quantize_mx(
                 out=hc[b][:, lo:hi].bitcast(FP8X4), scales=hs[b][:, lo:hi], in_=hg[b][:, 4 * lo : 4 * hi]
             )
 
-        def m2(b, hs_list):
-            lo, hi = hs_list[0] * 128, (hs_list[-1] + 1) * 128
+        def m2(b, part):
+            lo, hi = span(part)
             n = hi - lo
             bank = ps_b.tile([P, 2 * n], F32, name="bank_b")
-            l2[(b, hs_list[0])] = bank
+            l2[(b, part)] = bank
             for m in range(2):
                 nc.tensor.matmul_mx(
                     out=bank[:, m * n : (m + 1) * n],
@@ -176,93 +191,64 @@ def tile_cnn_pa_t_kernel(tc, x, w0, w1, out):
                     stop=True,
                 )
 
-        def eo(b, hs_list, eng):
+        def eo(b, part, eng):
             if b not in ot:
-                ot_b = outs.tile([P, 512], F32, name="ot%d" % b)
+                ot_b = hid.tile([P, 512], F32, name="ot%d" % b)
                 ot[b] = ot_b
-            lo, hi = hs_list[0] * 128, (hs_list[-1] + 1) * 128
+            lo, hi = span(part)
             dst = ot[b][:].rearrange("p (m r) -> p m r", m=2)[:, :, lo:hi]
-            relu_out(eng, dst, l2[(b, hs_list[0])][:].rearrange("p (m r) -> p m r", m=2), S2)
-            nc.sync.dma_start(out=out[b].rearrange("(i m) r -> i m r", m=2)[:, :, lo:hi], in_=dst)
+            relu_out(eng, dst, l2[(b, part)][:].rearrange("p (m r) -> p m r", m=2), S2)
+
+        def st(b, part):
+            lo, hi = span(part)
+            nc.sync.dma_start(
+                out=out[b].rearrange("(i m) r -> i m r", m=2)[:, :, lo:hi],
+                in_=ot[b][:].rearrange("p (m r) -> p m r", m=2)[:, :, lo:hi],
+            )
 
         w0w = w0r[:].bitcast(F32).rearrange("i (m g p u) -> i m g u p", m=2, g=2, u=2)
         w0gw = w0g[:].bitcast(F32).rearrange("p (g m i u) -> p g m i u", g=2, m=2, u=2)
         w1w = w1r[:].bitcast(F32).rearrange("i (m p u) -> i m u p", m=2, u=2)
         w1gw = w1g[:].bitcast(F32).rearrange("p (m i u) -> p m i u", m=2, u=2)
 
-        def tw0(g):
+        def transposes(key, pick):
             bank = ps_a.tile([P, 512], F32, name="bank_a")
-            tw[g] = bank
+            tw[key] = bank
             for m in range(2):
                 for u in range(2):
                     s = 2 * m + u
-                    nc.tensor.transpose(bank[:, s * P : (s + 1) * P], w0w[:, m, g, u, :], ident[:])
-
-        def ew0(g, eng):
-            copy_words(eng, w0gw[:, g], tw[g][:].rearrange("p (m u i) -> p m i u", m=2, u=2))
-
-        def tw1():
-            bank = ps_a.tile([P, 512], F32, name="bank_a")
-            tw[2] = bank
-            for m in range(2):
-                for u in range(2):
-                    s = 2 * m + u
-                    nc.tensor.transpose(bank[:, s * P : (s + 1) * P], w1w[:, m, u, :], ident[:])
-
-        def ew1(eng):
-            copy_words(eng, w1gw, tw[2][:].rearrange("p (m u i) -> p m i u", m=2, u=2))
-
-        def qw0():
-            nc.vector.quantize_mx(out=w0c[:].bitcast(FP8X4), scales=w0s[:], in_=w0g[:])
-
-        def qw1():
-            nc.vector.quantize_mx(out=w1c[:].bitcast(FP8X4), scales=w1s[:], in_=w1g[:])
+                    nc.tensor.transpose(bank[:, s * P : (s + 1) * P], pick(m, u), ident[:])
 
         ctx.enter_context(tc.manual_schedule())
-        BOTH = [0, 1]
-        tw0(0)
-        tw0(1)
-        ew0(0, "S")
-        ra(0)
-        ew0(1, "V")
-        rb(0)
-        rs(0)
-        qw0()
-        tw1()
-        ew1("S")
-        qx(0)
-        m1(0)
-        qx(1)
-        m1(1)
-        for p in range(1, BS):
-            ra(p)
-            rs(p)
-            rb(p)
-            qx(2 * p)
-            m1(2 * p)
-            qx(2 * p + 1)
-            m1(2 * p + 1)
-            if p == 1:
-                qw1()
-            eh(2 * p - 2, "S")
-            eh(2 * p - 1, "S")
-            if 2 <= p < BS - 1:
-                q2(p - 2, BOTH)
-                m2(p - 2, BOTH)
-            if 3 <= p < BS - 1:
-                eo(p - 3, BOTH, "S")
-        q2(5, BOTH)
-        m2(5, BOTH)
-        eo(4, BOTH, "V")
-        eh(14, "S")
-        q2(6, BOTH)
-        m2(6, BOTH)
-        eh(15, "V")
-        q2(7, [0])
-        m2(7, [0])
-        eo(5, BOTH, "S")
-        q2(7, [1])
-        m2(7, [1])
-        eo(6, BOTH, "S")
-        eo(7, [0], "S")
-        eo(7, [1], "V")
+        for kind, a, b, e in ORDER:
+            if kind == "r":
+                regroup(a, b, e)
+            elif kind == "qx":
+                quant_x(a, b * 512, (b + 1) * 512)
+            elif kind == "qxh":
+                h = 0 if e == "a" else 1
+                quant_x(a, b * 512 + h * 256, b * 512 + (h + 1) * 256)
+            elif kind == "m1":
+                m1(a)
+            elif kind == "eh":
+                eh(a, e)
+            elif kind == "q2":
+                q2(a, b)
+            elif kind == "m2":
+                m2(a, b)
+            elif kind == "eo":
+                eo(a, b, e)
+            elif kind == "st":
+                st(a, b)
+            elif kind == "tw0":
+                transposes(a, lambda m, u: w0w[:, m, a, u, :])
+            elif kind == "tw1":
+                transposes(2, lambda m, u: w1w[:, m, u, :])
+            elif kind == "ew0":
+                copy_words(e, w0gw[:, a], tw[a][:].rearrange("p (m u i) -> p m i u", m=2, u=2))
+            elif kind == "ew1":
+                copy_words(e, w1gw, tw[2][:].rearrange("p (m u i) -> p m i u", m=2, u=2))
+            elif kind == "qw0":
+                nc.vector.quantize_mx(out=w0c[:].bitcast(FP8X4), scales=w0s[:], in_=w0g[:])
+            elif kind == "qw1":
+                nc.vector.quantize_mx(out=w1c[:].bitcast(FP8X4), scales=w1s[:], in_=w1g[:])

@@ -21,43 +21,14 @@ FLOPS = 2 * BS * Q * HID * (2 * CIN) + 2 * BS * R * HID * (2 * HID)
 S1 = 1.0 / math.sqrt(float(CIN))
 S2 = 1.0 / math.sqrt(float(HID))
 
-LOADS = [("g", 0, 0), ("w0", 0, 0), ("g", 0, 1), ("w1", 0, 0), ("g", 1, 0), ("g", 1, 1), ("g", 2, 0), ("g", 2, 1), ("g", 3, 0), ("g", 3, 1), ("g", 4, 0), ("g", 4, 1), ("g", 5, 0), ("g", 5, 1), ("g", 6, 0), ("g", 6, 1), ("g", 7, 0), ("g", 7, 1)]
-ORDER = [
-    ("r", 0, 0, "V"), ("qx", 0, 0, ""), ("tw0", 0, 0, ""), ("tw0", 1, 0, ""), ("ew0", 0, 0, "S"), ("ew0", 1, 0, "S"),
-    ("r", 0, 1, "V"), ("qx", 0, 1, ""), ("tw1", 0, 0, ""), ("r", 1, 0, "V"), ("r", 1, 0, "S"), ("qw0", 0, 0, ""),
-    ("m1", 0, 0, ""), ("m1", 1, 0, ""), ("ew1", 0, 0, "S"), ("r", 1, 1, "V"), ("r", 1, 1, "S"), ("qx", 1, 0, ""),
-    ("r", 2, 0, "V"), ("r", 2, 0, "S"), ("eh", 0, 0, "S"), ("qx", 1, 1, ""), ("m1", 2, 0, ""), ("m1", 3, 0, ""),
-    ("r", 2, 1, "V"), ("r", 2, 1, "S"), ("eh", 1, 0, "S"), ("qx", 2, 0, ""), ("r", 3, 0, "V"), ("r", 3, 0, "S"),
-    ("eh", 2, 0, "S"), ("qx", 2, 1, ""), ("m1", 4, 0, ""), ("m1", 5, 0, ""), ("qw1", 0, 0, ""), ("r", 3, 1, "V"),
-    ("r", 3, 1, "S"), ("eh", 3, 0, "S"), ("qx", 3, 0, ""), ("r", 4, 0, "V"), ("r", 4, 0, "S"), ("eh", 4, 0, "S"),
-    ("qx", 3, 1, ""), ("m1", 6, 0, ""), ("m1", 7, 0, ""), ("q2", 0, 2, ""), ("m2", 0, 2, ""), ("r", 4, 1, "V"),
-    ("r", 4, 1, "S"), ("eh", 5, 0, "S"), ("qx", 4, 0, ""), ("r", 5, 0, "V"), ("r", 5, 0, "S"), ("eh", 6, 0, "S"),
-    ("qx", 4, 1, ""), ("m1", 8, 0, ""), ("m1", 9, 0, ""), ("q2", 1, 2, ""), ("m2", 1, 2, ""), ("r", 5, 1, "V"),
-    ("r", 5, 1, "S"), ("eh", 7, 0, "S"), ("qx", 5, 0, ""), ("eo", 0, 2, "S"), ("st", 0, 2, ""), ("r", 6, 0, "V"),
-    ("r", 6, 0, "S"), ("eh", 8, 0, "S"), ("qx", 5, 1, ""), ("m1", 10, 0, ""), ("m1", 11, 0, ""), ("q2", 2, 2, ""),
-    ("m2", 2, 2, ""), ("r", 6, 1, "V"), ("r", 6, 1, "S"), ("eh", 9, 0, "S"), ("qx", 6, 0, ""), ("r", 7, 0, "V"),
-    ("r", 7, 0, "S"), ("eh", 10, 0, "S"), ("qx", 6, 1, ""), ("m1", 12, 0, ""), ("m1", 13, 0, ""), ("q2", 3, 2, ""),
-    ("m2", 3, 2, ""), ("r", 7, 1, "V"), ("r", 7, 1, "S"), ("eh", 11, 0, "S"), ("qx", 7, 0, ""), ("qxh", 7, 1, "a"),
-    ("m1", 14, 0, ""), ("qxh", 7, 1, "b"), ("m1", 15, 0, ""), ("eo", 1, 2, "S"), ("eo", 2, 2, "V"), ("eh", 12, 0, "S"),
-    ("q2", 4, 2, ""), ("st", 1, 2, ""), ("eh", 13, 0, "S"), ("q2", 5, 2, ""), ("st", 2, 2, ""), ("eh", 14, 0, "S"),
-    ("eo", 3, 2, "V"), ("m2", 4, 2, ""), ("m2", 5, 2, ""), ("q2", 6, 2, ""), ("eh", 15, 0, "S"), ("eo", 4, 2, "V"),
-    ("st", 3, 2, ""), ("eo", 5, 2, "S"), ("m2", 6, 2, ""), ("q2", 7, 0, ""), ("q2", 7, 1, ""), ("st", 4, 2, ""),
-    ("m2", 7, 0, ""), ("eo", 6, 2, "S"), ("m2", 7, 1, ""), ("st", 5, 2, ""), ("eo", 7, 0, "S"), ("eo", 7, 1, "V"),
-    ("st", 6, 2, ""), ("st", 7, 0, ""), ("st", 7, 1, ""),
-]
-
-
-def scalar_words(b, g):
-    return 0 if b == 0 else (512 if (b == 7 and g == 1) else 384)
-
 
 def tile_cnn_pa_t_kernel(tc, x, w0, w1, out):
     nc = tc.nc
     with ExitStack() as ctx:
         const = ctx.enter_context(tc.tile_pool(name="const", bufs=1))
         raw = ctx.enter_context(tc.tile_pool(name="raw", bufs=1))
-        work = ctx.enter_context(tc.tile_pool(name="work", bufs=3))
-        hid = ctx.enter_context(tc.tile_pool(name="hid", bufs=1))
+        work = ctx.enter_context(tc.tile_pool(name="work", bufs=4))
+        outs = ctx.enter_context(tc.tile_pool(name="outs", bufs=1))
         ps_a = ctx.enter_context(tc.psum_pool(name="ps_a", bufs=5))
         ps_b = ctx.enter_context(tc.psum_pool(name="ps_b", bufs=3))
 
@@ -68,21 +39,26 @@ def tile_cnn_pa_t_kernel(tc, x, w0, w1, out):
         w0r = const.tile([P, 2048], BF16, name="w0r")
         w1r = const.tile([P, 1024], BF16, name="w1r")
 
-        for kind, b, g in LOADS:
-            if kind == "w0":
-                nc.sync.dma_start(out=w0r[:], in_=w0.rearrange("(i m) c k -> i (m c k)", m=2))
-            elif kind == "w1":
-                nc.sync.dma_start(out=w1r[:], in_=w1.rearrange("(i m) c k -> i (m c k)", m=2))
-            elif kind == "g":
-                nc.sync.dma_start(
-                    out=xr[b][:, g * 2048 : (g + 1) * 2048],
-                    in_=x[b].rearrange("(g p r) d -> g p (r d)", g=2, p=P, r=2)[g],
-                )
-            else:
-                nc.sync.dma_start(
-                    out=xr[b][:].rearrange("p (g n) -> p g n", g=2),
-                    in_=x[b].rearrange("(g p r) d -> p g (r d)", g=2, p=P, r=2),
-                )
+        def load_batch(b):
+            nc.sync.dma_start(
+                out=xr[b][:].rearrange("p (g n) -> p g n", g=2),
+                in_=x[b].rearrange("(g p r) d -> p g (r d)", g=2, p=P, r=2),
+            )
+
+        def load_half(b, g):
+            nc.sync.dma_start(
+                out=xr[b][:, g * 2048 : (g + 1) * 2048],
+                in_=x[b].rearrange("(g p r) d -> g p (r d)", g=2, p=P, r=2)[g],
+            )
+
+        nc.sync.dma_start(out=w0r[:], in_=w0.rearrange("(i m) c k -> i (m c k)", m=2))
+        load_half(0, 0)
+        load_half(0, 1)
+        nc.sync.dma_start(out=w1r[:], in_=w1.rearrange("(i m) c k -> i (m c k)", m=2))
+        for b in range(1, BS - 1):
+            load_batch(b)
+        load_half(BS - 1, 0)
+        load_half(BS - 1, 1)
 
         warm = const.tile([P, 1], F32, name="warm")
         nc.vector.memset(warm[:], 0.0)
@@ -111,15 +87,33 @@ def tile_cnn_pa_t_kernel(tc, x, w0, w1, out):
             else:
                 nc.vector.tensor_copy(out=dst, in_=src)
 
-        def regroup(b, g, eng):
+        def views(b):
             if b not in xg:
                 xg_b = work.tile([P, 4096], BF16, name="xg", align_bytes=64)
                 xg[b] = xg_b
-            cut = Q - scalar_words(b, g) // 2
-            lo, hi = (0, cut) if eng == "V" else (cut, Q)
-            src = xr[b][:].bitcast(F32).rearrange("p (g r q) -> p g q r", g=2, r=2)
-            dst = xg[b][:].bitcast(F32).rearrange("p (g q r) -> p g q r", g=2, r=2)
-            copy_words(eng, dst[:, g, lo:hi, :], src[:, g, lo:hi, :])
+            src = xr[b][:].bitcast(F32).rearrange("p (g r h q) -> p h g q r", g=2, r=2, h=2)
+            dst = xg[b][:].bitcast(F32).rearrange("p (h g q r) -> p h g q r", h=2, g=2, r=2)
+            return src, dst
+
+        def ra(b):
+            src, dst = views(b)
+            copy_words("V", dst[:, 0], src[:, 0])
+
+        def rb(b):
+            src, dst = views(b)
+            copy_words("V", dst[:, 1, 0], src[:, 1, 0])
+
+        def rs(b):
+            src, dst = views(b)
+            copy_words("S", dst[:, 1, 1], src[:, 1, 1])
+
+        def rg(b):
+            src, dst = views(b)
+            copy_words("V", dst[:, :, 0], src[:, :, 0])
+
+        def rc(b):
+            src, dst = views(b)
+            copy_words("V", dst[:, 0, 1], src[:, 0, 1])
 
         def quant_x(b, lo, hi):
             if b not in xc:
@@ -131,6 +125,13 @@ def tile_cnn_pa_t_kernel(tc, x, w0, w1, out):
                 out=xc[b][:, lo:hi].bitcast(FP8X4), scales=xs[b][:, lo:hi], in_=xg[b][:, 4 * lo : 4 * hi]
             )
 
+        def qx(c):
+            b, h = divmod(c, 2)
+            quant_x(b, h * 512, (h + 1) * 512)
+
+        def qxb(b, g, h):
+            quant_x(b, (2 * h + g) * 256, (2 * h + g + 1) * 256)
+
         def m1(c):
             b, h = divmod(c, 2)
             bank = ps_a.tile([P, 512], F32, name="bank_a")
@@ -138,7 +139,7 @@ def tile_cnn_pa_t_kernel(tc, x, w0, w1, out):
             for m in range(2):
                 for g in range(2):
                     wsl = slice((g * 2 + m) * P, (g * 2 + m + 1) * P)
-                    xsl = slice(g * 512 + h * 256, g * 512 + (h + 1) * 256)
+                    xsl = slice(h * 512 + g * 256, h * 512 + (g + 1) * 256)
                     nc.tensor.matmul_mx(
                         out=bank[:, m * 256 : (m + 1) * 256],
                         lhsT=w0c[:, wsl].bitcast(FP8X4),
@@ -151,8 +152,8 @@ def tile_cnn_pa_t_kernel(tc, x, w0, w1, out):
 
         def eh(c, eng):
             b, h = divmod(c, 2)
-            if b not in hg:
-                hg_b = hid.tile([P, 1024], BF16, name="hg%d" % b, align_bytes=64)
+            if h == 0:
+                hg_b = work.tile([P, 1024], BF16, name="hg", align_bytes=64)
                 hg[b] = hg_b
             relu_out(
                 eng,
@@ -161,25 +162,22 @@ def tile_cnn_pa_t_kernel(tc, x, w0, w1, out):
                 S1,
             )
 
-        def span(part):
-            return (0, 256) if part == 2 else (part * 128, (part + 1) * 128)
-
-        def q2(b, part):
+        def q2(b, hs_list):
             if b not in hc:
-                hc_b = hid.tile([P, 256], U32, name="hc%d" % b, align_bytes=64)
-                hs_b = hid.tile([P, 256], U8, name="hs%d" % b, align_bytes=64)
+                hc_b = work.tile([P, 256], U32, name="hc", align_bytes=64)
+                hs_b = work.tile([P, 256], U8, name="hs", align_bytes=64)
                 hc[b] = hc_b
                 hs[b] = hs_b
-            lo, hi = span(part)
+            lo, hi = hs_list[0] * 128, (hs_list[-1] + 1) * 128
             nc.vector.quantize_mx(
                 out=hc[b][:, lo:hi].bitcast(FP8X4), scales=hs[b][:, lo:hi], in_=hg[b][:, 4 * lo : 4 * hi]
             )
 
-        def m2(b, part):
-            lo, hi = span(part)
+        def m2(b, hs_list):
+            lo, hi = hs_list[0] * 128, (hs_list[-1] + 1) * 128
             n = hi - lo
             bank = ps_b.tile([P, 2 * n], F32, name="bank_b")
-            l2[(b, part)] = bank
+            l2[(b, hs_list[0])] = bank
             for m in range(2):
                 nc.tensor.matmul_mx(
                     out=bank[:, m * n : (m + 1) * n],
@@ -191,64 +189,104 @@ def tile_cnn_pa_t_kernel(tc, x, w0, w1, out):
                     stop=True,
                 )
 
-        def eo(b, part, eng):
+        def eo(b, hs_list, eng):
             if b not in ot:
-                ot_b = hid.tile([P, 512], F32, name="ot%d" % b)
+                ot_b = outs.tile([P, 512], F32, name="ot%d" % b)
                 ot[b] = ot_b
-            lo, hi = span(part)
+            lo, hi = hs_list[0] * 128, (hs_list[-1] + 1) * 128
             dst = ot[b][:].rearrange("p (m r) -> p m r", m=2)[:, :, lo:hi]
-            relu_out(eng, dst, l2[(b, part)][:].rearrange("p (m r) -> p m r", m=2), S2)
-
-        def st(b, part):
-            lo, hi = span(part)
-            nc.sync.dma_start(
-                out=out[b].rearrange("(i m) r -> i m r", m=2)[:, :, lo:hi],
-                in_=ot[b][:].rearrange("p (m r) -> p m r", m=2)[:, :, lo:hi],
-            )
+            relu_out(eng, dst, l2[(b, hs_list[0])][:].rearrange("p (m r) -> p m r", m=2), S2)
+            nc.sync.dma_start(out=out[b].rearrange("(i m) r -> i m r", m=2)[:, :, lo:hi], in_=dst)
 
         w0w = w0r[:].bitcast(F32).rearrange("i (m g p u) -> i m g u p", m=2, g=2, u=2)
         w0gw = w0g[:].bitcast(F32).rearrange("p (g m i u) -> p g m i u", g=2, m=2, u=2)
         w1w = w1r[:].bitcast(F32).rearrange("i (m p u) -> i m u p", m=2, u=2)
         w1gw = w1g[:].bitcast(F32).rearrange("p (m i u) -> p m i u", m=2, u=2)
 
-        def transposes(key, pick):
+        def tw0(g):
             bank = ps_a.tile([P, 512], F32, name="bank_a")
-            tw[key] = bank
+            tw[g] = bank
             for m in range(2):
                 for u in range(2):
                     s = 2 * m + u
-                    nc.tensor.transpose(bank[:, s * P : (s + 1) * P], pick(m, u), ident[:])
+                    nc.tensor.transpose(bank[:, s * P : (s + 1) * P], w0w[:, m, g, u, :], ident[:])
+
+        def ew0(g, eng):
+            copy_words(eng, w0gw[:, g], tw[g][:].rearrange("p (m u i) -> p m i u", m=2, u=2))
+
+        def tw1():
+            bank = ps_a.tile([P, 512], F32, name="bank_a")
+            tw[2] = bank
+            for m in range(2):
+                for u in range(2):
+                    s = 2 * m + u
+                    nc.tensor.transpose(bank[:, s * P : (s + 1) * P], w1w[:, m, u, :], ident[:])
+
+        def ew1(eng):
+            copy_words(eng, w1gw, tw[2][:].rearrange("p (m u i) -> p m i u", m=2, u=2))
+
+        def qw0():
+            nc.vector.quantize_mx(out=w0c[:].bitcast(FP8X4), scales=w0s[:], in_=w0g[:])
+
+        def qw1():
+            nc.vector.quantize_mx(out=w1c[:].bitcast(FP8X4), scales=w1s[:], in_=w1g[:])
 
         ctx.enter_context(tc.manual_schedule())
-        for kind, a, b, e in ORDER:
-            if kind == "r":
-                regroup(a, b, e)
-            elif kind == "qx":
-                quant_x(a, b * 512, (b + 1) * 512)
-            elif kind == "qxh":
-                h = 0 if e == "a" else 1
-                quant_x(a, b * 512 + h * 256, b * 512 + (h + 1) * 256)
-            elif kind == "m1":
-                m1(a)
-            elif kind == "eh":
-                eh(a, e)
-            elif kind == "q2":
-                q2(a, b)
-            elif kind == "m2":
-                m2(a, b)
-            elif kind == "eo":
-                eo(a, b, e)
-            elif kind == "st":
-                st(a, b)
-            elif kind == "tw0":
-                transposes(a, lambda m, u: w0w[:, m, a, u, :])
-            elif kind == "tw1":
-                transposes(2, lambda m, u: w1w[:, m, u, :])
-            elif kind == "ew0":
-                copy_words(e, w0gw[:, a], tw[a][:].rearrange("p (m u i) -> p m i u", m=2, u=2))
-            elif kind == "ew1":
-                copy_words(e, w1gw, tw[2][:].rearrange("p (m u i) -> p m i u", m=2, u=2))
-            elif kind == "qw0":
-                nc.vector.quantize_mx(out=w0c[:].bitcast(FP8X4), scales=w0s[:], in_=w0g[:])
-            elif kind == "qw1":
-                nc.vector.quantize_mx(out=w1c[:].bitcast(FP8X4), scales=w1s[:], in_=w1g[:])
+        BOTH = [0, 1]
+        tw0(0)
+        tw0(1)
+        ew0(0, "S")
+        ew0(1, "S")
+        rg(0)
+        rc(0)
+        rs(0)
+        tw1()
+        ew1("S")
+        qw0()
+        qx(0)
+        m1(0)
+        qx(1)
+        m1(1)
+        for p in range(1, BS):
+            if p < BS - 1:
+                ra(p)
+                rs(p)
+                rb(p)
+                qx(2 * p)
+                m1(2 * p)
+                qx(2 * p + 1)
+                m1(2 * p + 1)
+            else:
+                rg(p)
+                q2(5, BOTH)
+                m2(5, BOTH)
+                qxb(p, 0, 0)
+                rs(p)
+                rc(p)
+                qxb(p, 0, 1)
+                qxb(p, 1, 0)
+                m1(2 * p)
+                qxb(p, 1, 1)
+                m1(2 * p + 1)
+            if p == 1:
+                qw1()
+            eh(2 * p - 2, "S")
+            eh(2 * p - 1, "S")
+            if 2 <= p < BS - 1:
+                q2(p - 2, BOTH)
+                m2(p - 2, BOTH)
+            if 3 <= p < BS - 1:
+                eo(p - 3, BOTH, "S")
+        eo(4, BOTH, "V")
+        eh(14, "S")
+        q2(6, BOTH)
+        m2(6, BOTH)
+        eh(15, "V")
+        q2(7, [0])
+        m2(7, [0])
+        eo(5, BOTH, "S")
+        q2(7, [1])
+        m2(7, [1])
+        eo(6, BOTH, "S")
+        eo(7, [0], "S")
+        eo(7, [1], "V")

@@ -251,6 +251,9 @@ def tile_cnn_pa_t_kernel(tc, x, w0, w1, out):
             if p < BS - 1:
                 ra(p)
                 rs(p)
+                if p >= 2:
+                    q2(p - 2, BOTH)
+                    m2(p - 2, BOTH)
                 rb(p)
                 qx(2 * p)
                 m1(2 * p)
@@ -272,9 +275,6 @@ def tile_cnn_pa_t_kernel(tc, x, w0, w1, out):
                 qw1()
             eh(2 * p - 2, "S")
             eh(2 * p - 1, "S")
-            if 2 <= p < BS - 1:
-                q2(p - 2, BOTH)
-                m2(p - 2, BOTH)
             if 3 <= p < BS - 1:
                 eo(p - 3, BOTH, "S")
         eo(4, BOTH, "V")

@@ -20,6 +20,7 @@ R = Q // 2
 FLOPS = 2 * BS * Q * HID * (2 * CIN) + 2 * BS * R * HID * (2 * HID)
 S1 = 1.0 / math.sqrt(float(CIN))
 S2 = 1.0 / math.sqrt(float(HID))
+QS = 192
 
 
 def tile_cnn_pa_t_kernel(tc, x, w0, w1, out):
@@ -101,7 +102,11 @@ def tile_cnn_pa_t_kernel(tc, x, w0, w1, out):
 
         def rb(b):
             src, dst = views(b)
-            copy_words("V", dst[:, 1, 0], src[:, 1, 0])
+            copy_words("V", dst[:, 1, 0, 0:QS], src[:, 1, 0, 0:QS])
+
+        def rt(b):
+            src, dst = views(b)
+            copy_words("S", dst[:, 1, 0, QS:256], src[:, 1, 0, QS:256])
 
         def rs(b):
             src, dst = views(b)
@@ -251,6 +256,7 @@ def tile_cnn_pa_t_kernel(tc, x, w0, w1, out):
             if p < BS - 1:
                 ra(p)
                 rs(p)
+                rt(p)
                 if p >= 2:
                     q2(p - 2, BOTH)
                     m2(p - 2, BOTH)
@@ -275,16 +281,14 @@ def tile_cnn_pa_t_kernel(tc, x, w0, w1, out):
                 qw1()
             eh(2 * p - 2, "S")
             eh(2 * p - 1, "S")
-            if 3 <= p < BS - 1:
-                eo(p - 3, BOTH, "S")
-        eo(4, BOTH, "V")
+            if p >= 2:
+                eo(p - 2, BOTH, "S")
         eh(14, "S")
         q2(6, BOTH)
         m2(6, BOTH)
         eh(15, "V")
         q2(7, [0])
         m2(7, [0])
-        eo(5, BOTH, "S")
         q2(7, [1])
         m2(7, [1])
         eo(6, BOTH, "S")

@@ -20,7 +20,7 @@ R = Q // 2
 FLOPS = 2 * BS * Q * HID * (2 * CIN) + 2 * BS * R * HID * (2 * HID)
 S1 = 1.0 / math.sqrt(float(CIN))
 S2 = 1.0 / math.sqrt(float(HID))
-QS = 192
+QS = 96
 
 
 def tile_cnn_pa_t_kernel(tc, x, w0, w1, out):
@@ -102,11 +102,11 @@ def tile_cnn_pa_t_kernel(tc, x, w0, w1, out):
 
         def rb(b):
             src, dst = views(b)
-            copy_words("V", dst[:, 1, 0, 0:QS], src[:, 1, 0, 0:QS])
+            copy_words("V", dst[:, 1, :, 0:QS], src[:, 1, :, 0:QS])
 
         def rt(b):
             src, dst = views(b)
-            copy_words("S", dst[:, 1, 0, QS:256], src[:, 1, 0, QS:256])
+            copy_words("S", dst[:, 1, :, QS:256], src[:, 1, :, QS:256])
 
         def rs(b):
             src, dst = views(b)
@@ -255,7 +255,6 @@ def tile_cnn_pa_t_kernel(tc, x, w0, w1, out):
         for p in range(1, BS):
             if p < BS - 1:
                 ra(p)
-                rs(p)
                 rt(p)
                 if p >= 2:
                     q2(p - 2, BOTH)

@@ -120,6 +120,10 @@ def tile_cnn_pa_t_kernel(tc, x, w0, w1, out):
             src, dst = views(b)
             copy_words("V", dst[:, 0, 1], src[:, 0, 1])
 
+        def rblock(eng, b, h, g):
+            src, dst = views(b)
+            copy_words(eng, dst[:, h, g], src[:, h, g])
+
         def quant_x(b, lo, hi):
             if b not in xc:
                 xc_b = work.tile([P, 1024], U32, name="xc", align_bytes=64)
@@ -265,7 +269,8 @@ def tile_cnn_pa_t_kernel(tc, x, w0, w1, out):
                 qx(2 * p + 1)
                 m1(2 * p + 1)
             else:
-                rg(p)
+                rblock("V", p, 0, 0)
+                rblock("S", p, 1, 0)
                 q2(5, BOTH)
                 m2(5, BOTH)
                 qxb(p, 0, 0)

@@ -141,23 +141,33 @@ def tile_cnn_pa_t_kernel(tc, x, w0, w1, out):
         def qxb(b, g, h):
             quant_x(b, (2 * h + g) * 256, (2 * h + g + 1) * 256)
 
-        def m1(c):
+        def l1_pass(c, m, g):
             b, h = divmod(c, 2)
+            wsl = slice((g * 2 + m) * P, (g * 2 + m + 1) * P)
+            xsl = slice(h * 512 + g * 256, h * 512 + (g + 1) * 256)
+            nc.tensor.matmul_mx(
+                out=l1[c][:, m * 256 : (m + 1) * 256],
+                lhsT=w0c[:, wsl].bitcast(FP8X4),
+                lhsT_scale=w0s[:, wsl],
+                rhs=xc[b][:, xsl].bitcast(FP8X4),
+                rhs_scale=xs[b][:, xsl],
+                start=(g == 0),
+                stop=(g == 1),
+            )
+
+        def m1_open(c):
             bank = ps_a.tile([P, 512], F32, name="bank_a")
             l1[c] = bank
-            for m in range(2):
-                for g in range(2):
-                    wsl = slice((g * 2 + m) * P, (g * 2 + m + 1) * P)
-                    xsl = slice(h * 512 + g * 256, h * 512 + (g + 1) * 256)
-                    nc.tensor.matmul_mx(
-                        out=bank[:, m * 256 : (m + 1) * 256],
-                        lhsT=w0c[:, wsl].bitcast(FP8X4),
-                        lhsT_scale=w0s[:, wsl],
-                        rhs=xc[b][:, xsl].bitcast(FP8X4),
-                        rhs_scale=xs[b][:, xsl],
-                        start=(g == 0),
-                        stop=(g == 1),
-                    )
+            l1_pass(c, 0, 0)
+
+        def m1_close(c):
+            l1_pass(c, 0, 1)
+            l1_pass(c, 1, 0)
+            l1_pass(c, 1, 1)
+
+        def m1(c):
+            m1_open(c)
+            m1_close(c)
 
         def eh(c, eng):
             b, h = divmod(c, 2)
@@ -274,13 +284,15 @@ def tile_cnn_pa_t_kernel(tc, x, w0, w1, out):
                 q2(5, BOTH)
                 m2(5, BOTH)
                 qxb(p, 0, 0)
+                m1_open(2 * p)
                 rs(p)
                 rc(p)
                 qxb(p, 0, 1)
+                m1_open(2 * p + 1)
                 qxb(p, 1, 0)
-                m1(2 * p)
+                m1_close(2 * p)
                 qxb(p, 1, 1)
-                m1(2 * p + 1)
+                m1_close(2 * p + 1)
             if p == 1:
                 qw1()
             eh(2 * p - 2, "S")

@@ -215,7 +215,8 @@ def tile_cnn_pa_t_kernel(tc, x, w0, w1, out):
             lo, hi = hs_list[0] * 128, (hs_list[-1] + 1) * 128
             dst = ot[b][:].rearrange("p (m r) -> p m r", m=2)[:, :, lo:hi]
             relu_out(eng, dst, l2[(b, hs_list[0])][:].rearrange("p (m r) -> p m r", m=2), S2)
-            nc.sync.dma_start(out=out[b].rearrange("(i m) r -> i m r", m=2)[:, :, lo:hi], in_=dst)
+            if hi == R:
+                nc.sync.dma_start(out=out[b].rearrange("(i m) r -> i (m r)", m=2), in_=ot[b][:])
 
         w0w = w0r[:].bitcast(F32).rearrange("i (m g p u) -> i m g u p", m=2, g=2, u=2)
         w0gw = w0g[:].bitcast(F32).rearrange("p (g m i u) -> p g m i u", g=2, m=2, u=2)

import math
from contextlib import ExitStack

import concourse.mybir as mybir
from concourse.masks import make_identity

F32 = mybir.dt.float32
BF16 = mybir.dt.bfloat16
U32 = mybir.dt.uint32
U8 = mybir.dt.uint8
FP8X4 = mybir.dt.float8_e4m3fn_x4
RELU = mybir.ActivationFunctionType.Relu
MULT = mybir.AluOpType.mult
MAX = mybir.AluOpType.max

P = 128
BS, CIN, HID, D = 8, 512, 256, 1024
Q = D // 2
R = Q // 2
FLOPS = 2 * BS * Q * HID * (2 * CIN) + 2 * BS * R * HID * (2 * HID)
S1 = 1.0 / math.sqrt(float(CIN))
S2 = 1.0 / math.sqrt(float(HID))
QS = 96


def tile_cnn_pa_t_kernel(tc, x, w0, w1, out):
    nc = tc.nc
    with ExitStack() as ctx:
        const = ctx.enter_context(tc.tile_pool(name="const", bufs=1))
        raw = ctx.enter_context(tc.tile_pool(name="raw", bufs=1))
        work = ctx.enter_context(tc.tile_pool(name="work", bufs=4))
        outs = ctx.enter_context(tc.tile_pool(name="outs", bufs=1))
        ps_a = ctx.enter_context(tc.psum_pool(name="ps_a", bufs=5))
        ps_b = ctx.enter_context(tc.psum_pool(name="ps_b", bufs=3))

        xr = []
        for b in range(BS):
            xr_b = raw.tile([P, 4096], BF16, name="xr%d" % b)
            xr.append(xr_b)
        w0r = const.tile([P, 2048], BF16, name="w0r")
        w1r = const.tile([P, 1024], BF16, name="w1r")

        def load_batch(b):
            nc.sync.dma_start(
                out=xr[b][:].rearrange("p (g n) -> p g n", g=2),
                in_=x[b].rearrange("(g p r) d -> p g (r d)", g=2, p=P, r=2),
            )

        def load_half(b, g):
            nc.sync.dma_start(
                out=xr[b][:, g * 2048 : (g + 1) * 2048],
                in_=x[b].rearrange("(g p r) d -> g p (r d)", g=2, p=P, r=2)[g],
            )

        nc.sync.dma_start(out=w0r[:], in_=w0.rearrange("(i m) c k -> i (m c k)", m=2))
        load_half(0, 0)
        load_half(0, 1)
        nc.sync.dma_start(out=w1r[:], in_=w1.rearrange("(i m) c k -> i (m c k)", m=2))
        for b in range(1, BS - 1):
            load_batch(b)
        load_half(BS - 1, 0)
        load_half(BS - 1, 1)

        warm = const.tile([P, 1], F32, name="warm")
        nc.vector.memset(warm[:], 0.0)
        nc.scalar.activation(out=warm[:], in_=warm[:], func=RELU)
        ident = const.tile([P, P], F32, name="ident")
        make_identity(nc, ident[:])

        w0g = const.tile([P, 2048], BF16, name="w0g", align_bytes=64)
        w0c = const.tile([P, 512], U32, name="w0c", align_bytes=64)
        w0s = const.tile([P, 512], U8, name="w0s", align_bytes=64)
        w1g = const.tile([P, 1024], BF16, name="w1g", align_bytes=64)
        w1c = const.tile([P, 256], U32, name="w1c", align_bytes=64)
        w1s = const.tile([P, 256], U8, name="w1s", align_bytes=64)

        xg, xc, xs, hg, hc, hs, l1, l2, ot, tw = {}, {}, {}, {}, {}, {}, {}, {}, {}, {}

        def relu_out(eng, dst, src, scale):
            if eng == "S":
                nc.scalar.activation(out=dst, in_=src, func=RELU, scale=scale)
            else:
                nc.vector.tensor_scalar(out=dst, in0=src, scalar1=scale, scalar2=0.0, op0=MULT, op1=MAX)

        def copy_words(eng, dst, src):
            if eng == "S":
                nc.scalar.copy(out=dst, in_=src)
            else:
                nc.vector.tensor_copy(out=dst, in_=src)

        def views(b):
            if b not in xg:
                xg_b = work.tile([P, 4096], BF16, name="xg", align_bytes=64)
                xg[b] = xg_b
            src = xr[b][:].bitcast(F32).rearrange("p (g r h q) -> p h g q r", g=2, r=2, h=2)
            dst = xg[b][:].bitcast(F32).rearrange("p (h g q r) -> p h g q r", h=2, g=2, r=2)
            return src, dst

        def ra(b):
            src, dst = views(b)
            copy_words("V", dst[:, 0], src[:, 0])

        def rb(b):
            src, dst = views(b)
            copy_words("V", dst[:, 1, :, 0:QS], src[:, 1, :, 0:QS])

        def rt(b):
            src, dst = views(b)
            copy_words("S", dst[:, 1, :, QS:256], src[:, 1, :, QS:256])

        def rs(b):
            src, dst = views(b)
            copy_words("S", dst[:, 1, 1], src[:, 1, 1])

        def rg(b):
            src, dst = views(b)
            copy_words("V", dst[:, :, 0], src[:, :, 0])

        def rc(b):
            src, dst = views(b)
            copy_words("V", dst[:, 0, 1], src[:, 0, 1])

        def rblock(eng, b, h, g):
            src, dst = views(b)
            copy_words(eng, dst[:, h, g], src[:, h, g])

        def quant_x(b, lo, hi):
            if b not in xc:
                xc_b = work.tile([P, 1024], U32, name="xc", align_bytes=64)
                xs_b = work.tile([P, 1024], U8, name="xs", align_bytes=64)
                xc[b] = xc_b
                xs[b] = xs_b
            nc.vector.quantize_mx(
                out=xc[b][:, lo:hi].bitcast(FP8X4), scales=xs[b][:, lo:hi], in_=xg[b][:, 4 * lo : 4 * hi]
            )

        def qx(c):
            b, h = divmod(c, 2)
            quant_x(b, h * 512, (h + 1) * 512)

        def qxb(b, g, h):
            quant_x(b, (2 * h + g) * 256, (2 * h + g + 1) * 256)

        def l1_pass(c, m, g):
            b, h = divmod(c, 2)
            wsl = slice((g * 2 + m) * P, (g * 2 + m + 1) * P)
            xsl = slice(h * 512 + g * 256, h * 512 + (g + 1) * 256)
            nc.tensor.matmul_mx(
                out=l1[c][:, m * 256 : (m + 1) * 256],
                lhsT=w0c[:, wsl].bitcast(FP8X4),
                lhsT_scale=w0s[:, wsl],
                rhs=xc[b][:, xsl].bitcast(FP8X4),
                rhs_scale=xs[b][:, xsl],
                start=(g == 0),
                stop=(g == 1),
            )

        def m1_open(c):
            bank = ps_a.tile([P, 512], F32, name="bank_a")
            l1[c] = bank
            l1_pass(c, 0, 0)

        def m1_close(c):
            l1_pass(c, 0, 1)
            l1_pass(c, 1, 0)
            l1_pass(c, 1, 1)

        def m1(c):
            m1_open(c)
            m1_close(c)

        def eh(c, eng):
            b, h = divmod(c, 2)
            if h == 0:
                hg_b = work.tile([P, 1024], BF16, name="hg", align_bytes=64)
                hg[b] = hg_b
            relu_out(
                eng,
                hg[b][:, h * 512 : (h + 1) * 512].rearrange("p (r m e) -> p r m e", m=2, e=2),
                l1[c][:].rearrange("p (m r e) -> p r m e", m=2, e=2),
                S1,
            )

        def q2(b, hs_list):
            if b not in hc:
                hc_b = work.tile([P, 256], U32, name="hc", align_bytes=64)
                hs_b = work.tile([P, 256], U8, name="hs", align_bytes=64)
                hc[b] = hc_b
                hs[b] = hs_b
            lo, hi = hs_list[0] * 128, (hs_list[-1] + 1) * 128
            nc.vector.quantize_mx(
                out=hc[b][:, lo:hi].bitcast(FP8X4), scales=hs[b][:, lo:hi], in_=hg[b][:, 4 * lo : 4 * hi]
            )

        def m2(b, hs_list):
            lo, hi = hs_list[0] * 128, (hs_list[-1] + 1) * 128
            n = hi - lo
            bank = ps_b.tile([P, 2 * n], F32, name="bank_b")
            l2[(b, hs_list[0])] = bank
            for m in range(2):
                nc.tensor.matmul_mx(
                    out=bank[:, m * n : (m + 1) * n],
                    lhsT=w1c[:, m * P : (m + 1) * P].bitcast(FP8X4),
                    lhsT_scale=w1s[:, m * P : (m + 1) * P],
                    rhs=hc[b][:, lo:hi].bitcast(FP8X4),
                    rhs_scale=hs[b][:, lo:hi],
                    start=True,
                    stop=True,
                )

        def eo(b, hs_list, eng):
            if b not in ot:
                ot_b = outs.tile([P, 512], F32, name="ot%d" % b)
                ot[b] = ot_b
            lo, hi = hs_list[0] * 128, (hs_list[-1] + 1) * 128
            dst = ot[b][:].rearrange("p (m r) -> p m r", m=2)[:, :, lo:hi]
            relu_out(eng, dst, l2[(b, hs_list[0])][:].rearrange("p (m r) -> p m r", m=2), S2)
            if hi == R:
                nc.sync.dma_start(out=out[b].rearrange("(i m) r -> i (m r)", m=2), in_=ot[b][:])

        w0w = w0r[:].bitcast(F32).rearrange("i (m g p u) -> i m g u p", m=2, g=2, u=2)
        w0gw = w0g[:].bitcast(F32).rearrange("p (g m i u) -> p g m i u", g=2, m=2, u=2)
        w1w = w1r[:].bitcast(F32).rearrange("i (m p u) -> i m u p", m=2, u=2)
        w1gw = w1g[:].bitcast(F32).rearrange("p (m i u) -> p m i u", m=2, u=2)

        def tw0(g):
            bank = ps_a.tile([P, 512], F32, name="bank_a")
            tw[g] = bank
            for m in range(2):
                for u in range(2):
                    s = 2 * m + u
                    nc.tensor.transpose(bank[:, s * P : (s + 1) * P], w0w[:, m, g, u, :], ident[:])

        def ew0(g, eng):
            copy_words(eng, w0gw[:, g], tw[g][:].rearrange("p (m u i) -> p m i u", m=2, u=2))

        def tw1():
            bank = ps_a.tile([P, 512], F32, name="bank_a")
            tw[2] = bank
            for m in range(2):
                for u in range(2):
                    s = 2 * m + u
                    nc.tensor.transpose(bank[:, s * P : (s + 1) * P], w1w[:, m, u, :], ident[:])

        def ew1(eng):
            copy_words(eng, w1gw, tw[2][:].rearrange("p (m u i) -> p m i u", m=2, u=2))

        def qw0():
            nc.vector.quantize_mx(out=w0c[:].bitcast(FP8X4), scales=w0s[:], in_=w0g[:])

        def qw1():
            nc.vector.quantize_mx(out=w1c[:].bitcast(FP8X4), scales=w1s[:], in_=w1g[:])

        ctx.enter_context(tc.manual_schedule())
        BOTH = [0, 1]
        tw0(0)
        tw0(1)
        ew0(0, "S")
        ew0(1, "S")
        rg(0)
        rc(0)
        rs(0)
        tw1()
        ew1("S")
        qw0()
        qx(0)
        m1(0)
        qx(1)
        m1(1)
        for p in range(1, BS):
            if p < BS - 1:
                ra(p)
                rt(p)
                if p >= 2:
                    q2(p - 2, BOTH)
                    m2(p - 2, BOTH)
                rb(p)
                qx(2 * p)
                m1(2 * p)
                qx(2 * p + 1)
                m1(2 * p + 1)
            else:
                rblock("V", p, 0, 0)
                rblock("S", p, 1, 0)
                q2(5, BOTH)
                m2(5, BOTH)
                qxb(p, 0, 0)
                m1_open(2 * p)
                rs(p)
                rc(p)
                qxb(p, 0, 1)
                m1_open(2 * p + 1)
                qxb(p, 1, 0)
                m1_close(2 * p)
                qxb(p, 1, 1)
                m1_close(2 * p + 1)
            if p == 1:
                qw1()
            eh(2 * p - 2, "S")
            eh(2 * p - 1, "S")
            if p >= 2:
                eo(p - 2, BOTH, "S")
        eh(14, "S")
        q2(6, BOTH)
        m2(6, BOTH)
        eh(15, "V")
        q2(7, [0])
        m2(7, [0])
        q2(7, [1])
        m2(7, [1])
        eo(6, BOTH, "S")
        eo(7, [0], "S")
        eo(7, [1], "V")
